import numpy as np
import ml_dtypes


def mxq(x, axis, fmt="e4m3"):
    dtype, down = {"e4m3": (ml_dtypes.float8_e4m3fn, 7), "e5m2": (ml_dtypes.float8_e5m2, 14)}[fmt]
    v = np.moveaxis(np.asarray(x, np.float32).astype(ml_dtypes.bfloat16).astype(np.float64), axis, -1)
    blocks = v.reshape(v.shape[:-1] + (-1, 32))
    amax = np.abs(blocks).max(-1, keepdims=True)
    byte = np.maximum(np.where(amax > 0, np.frexp(amax)[1] - 1 + 127, 0) - down, 1)
    scale = np.exp2(byte - 127.0)
    codes = (blocks / scale).astype(np.float32).astype(dtype).astype(np.float64)
    return np.moveaxis((codes * scale).reshape(v.shape), -1, axis)


WIDE = False


def mx_kscale(k):
    if not WIDE:
        return np.ones(k)
    levels = np.array([10, -10, 5, -5, 0])
    a = np.random.permutation(np.resize(levels, k // 512 * 4)).reshape(k // 512, 4)
    idx = np.arange(k)
    return np.exp2(a[idx // 512, idx % 128 // 32])


BF16 = ml_dtypes.bfloat16


def bf(x):
    return np.asarray(x, np.float32).astype(BF16)


def f64(x):
    return np.asarray(x).astype(np.float64)


SL, BS, DM, H, NH, DO = 64, 128, 1024, 4, 64, 1024
DP = H * NH


def log_softmax0(x):
    z = x - x.max(0, keepdims=True)
    return z - np.log(np.exp(z).sum(0, keepdims=True))


def setup_inputs():
    s, u = mx_kscale(DM), mx_kscale(DM)
    return {"query": bf(np.random.standard_normal((BS, DM)) * 2.0 * s),
            "keys": bf(np.random.standard_normal((SL, BS, DM)) * u),
            "Wq": bf(np.random.standard_normal((DP, DM)) / np.sqrt(DM) / s),
            "Wk": bf(np.random.standard_normal((DP, DM)) / np.sqrt(DM) / u)}


def reference(query, keys, Wq, Wk):
    qp = mxq(f64(query), 1, "e4m3") @ mxq(f64(Wq), 1, "e4m3").T
    kp = mxq(f64(keys), 2, "e4m3") @ mxq(f64(Wk), 1, "e4m3").T
    dot = (qp * kp).reshape(SL, BS, H, NH).sum(-1) / np.sqrt(NH)
    return log_softmax0(dot)

@@ -1,0 +1,238 @@
+import math
+from contextlib import ExitStack
+
+import concourse.mybir as mybir
+from concourse.masks import make_identity
+
+F32 = mybir.dt.float32
+BF16 = mybir.dt.bfloat16
+U32 = mybir.dt.uint32
+U8 = mybir.dt.uint8
+FP8X4 = mybir.dt.float8_e4m3fn_x4
+ALU = mybir.AluOpType
+ACT = mybir.ActivationFunctionType
+AXIS = mybir.AxisListType
+
+SL, BS, DM, H, NH = 64, 128, 1024, 4, 64
+DP = H * NH
+P = 128
+PACK = 4
+K_PASS = P * PACK
+PASSES = DM // K_PASS
+WORDS = DM // 2
+CHUNKS = WORDS // P
+HALVES = CHUNKS // PASSES
+S_LOAD = 2
+S_ROUND = 4
+ROUNDS = SL // S_ROUND
+S_BANK = 512 // DP
+
+FLOPS = 2 * (SL + 1) * BS * DM * DP
+
+
+def transpose_rows(nc, banks, ident, row_words):
+    bank = banks.tile([P, CHUNKS, P], F32)
+    for c in range(CHUNKS):
+        nc.tensor.transpose(bank[:, c, :], row_words[:, c * P : (c + 1) * P], ident[:])
+    return bank
+
+
+def by_pass_row_half(bank):
+    return bank[:].rearrange("p (g u) r -> p g r u", u=HALVES)
+
+
+def tile_multiheadattention_pa_t_kernel(tc, query, keys, Wq, Wk, out):
+    nc = tc.nc
+    with ExitStack() as ctx:
+        const = ctx.enter_context(tc.tile_pool(name="const", bufs=1))
+        resident = ctx.enter_context(tc.tile_pool(name="resident", bufs=SL // S_LOAD))
+        stage = ctx.enter_context(tc.tile_pool(name="stage", bufs=3))
+        banks = ctx.enter_context(tc.psum_pool(name="banks", bufs=4))
+        sums = ctx.enter_context(tc.psum_pool(name="sums", bufs=4))
+        ctx.enter_context(tc.manual_schedule())
+
+        key_rows = []
+
+        def load_keys(first, last):
+            for i in range(first, last):
+                rows = resident.tile([P, S_LOAD * DM], BF16, name="rows")
+                nc.sync.dma_start(
+                    out=rows[:].rearrange("b (s k) -> b s k", s=S_LOAD),
+                    in_=keys[i * S_LOAD : (i + 1) * S_LOAD].rearrange("s b k -> b s k"),
+                )
+                key_rows.append(rows)
+
+        loads_per_round = S_ROUND // S_LOAD
+        wk_rows = const.tile([P, (DP // P) * DM], BF16)
+        wq_rows = const.tile([P, (DP // P) * DM], BF16)
+        q_rows = const.tile([P, DM], BF16)
+        load_keys(0, loads_per_round)
+        nc.sync.dma_start(
+            out=wk_rows[:].rearrange("p (r k) -> p r k", k=DM),
+            in_=Wk.rearrange("(r p) k -> p r k", p=P),
+        )
+        load_keys(loads_per_round, 2 * loads_per_round)
+        nc.sync.dma_start(out=q_rows[:], in_=query)
+        nc.sync.dma_start(
+            out=wq_rows[:].rearrange("p (r k) -> p r k", k=DM),
+            in_=Wq.rearrange("(r p) k -> p r k", p=P),
+        )
+        load_keys(2 * loads_per_round, SL // S_LOAD)
+
+        ident = const.tile([P, P], F32)
+        make_identity(nc, ident[:])
+        one = const.tile([P, 1], F32)
+        nc.vector.memset(one[:], 1.0)
+        warm = const.tile([P, 1], F32)
+        nc.scalar.activation(out=warm[:], in_=one[:], func=ACT.Ln)
+        dot = const.tile([P, H, SL], F32)
+        result = const.tile([P, (H + 1) * SL], F32)
+        nc.gpsimd.memset(result[:, H * SL :], 0.0)
+
+        def quantise_weight(w_rows, name):
+            grouped = const.tile([P, PASSES * DP * PACK], BF16, align_bytes=64, name=name + "_grouped")
+            words = grouped[:].bitcast(F32).rearrange(
+                "p (g r c u) -> p g r c u", g=PASSES, r=DP // P, u=HALVES
+            )
+            for r in range(DP // P):
+                bank = transpose_rows(nc, banks, ident, w_rows[:].bitcast(F32)[:, r * WORDS : (r + 1) * WORDS])
+                nc.vector.tensor_copy(out=words[:, :, r, :, :], in_=by_pass_row_half(bank))
+            codes = const.tile([P, PASSES * DP], U32, align_bytes=64, name=name + "_codes")
+            scales = const.tile([P, PASSES * DP], U8, align_bytes=64, name=name + "_scales")
+            nc.vector.quantize_mx(out=codes[:].bitcast(FP8X4), scales=scales[:], in_=grouped[:])
+            return codes, scales
+
+        def project(acc, row_codes, row_scales, first_col, w_codes, w_scales):
+            for g in range(PASSES):
+                rows = slice(first_col + g * P, first_col + (g + 1) * P)
+                chans = slice(g * DP, (g + 1) * DP)
+                nc.tensor.matmul_mx(
+                    out=acc,
+                    lhsT=row_codes[:, rows].bitcast(FP8X4),
+                    lhsT_scale=row_scales[:, rows],
+                    rhs=w_codes[:, chans].bitcast(FP8X4),
+                    rhs_scale=w_scales[:, chans],
+                    start=(g == 0),
+                    stop=(g == PASSES - 1),
+                )
+
+        def project_query():
+            wq_codes, wq_scales = quantise_weight(wq_rows, "wq")
+            grouped = const.tile([P, DM], BF16, align_bytes=64, name="q_grouped")
+            bank = transpose_rows(nc, banks, ident, q_rows[:].bitcast(F32))
+            nc.vector.tensor_copy(
+                out=grouped[:].bitcast(F32).rearrange("p (g r u) -> p g r u", g=PASSES, u=HALVES),
+                in_=by_pass_row_half(bank),
+            )
+            codes = const.tile([P, PASSES * P], U32, align_bytes=64, name="q_codes")
+            scales = const.tile([P, PASSES * P], U8, align_bytes=64, name="q_scales")
+            nc.vector.quantize_mx(out=codes[:].bitcast(FP8X4), scales=scales[:], in_=grouped[:])
+            acc = sums.tile([P, S_BANK * DP], F32, name="acc")
+            project(acc[:, :DP], codes, scales, 0, wq_codes, wq_scales)
+            qp = const.tile([P, DP], F32)
+            nc.scalar.mul(out=qp[:], in_=acc[:, :DP], mul=1.0 / math.sqrt(NH))
+            return qp
+
+        grouped_of = {}
+        codes_of = {}
+        acc_of = {}
+
+        def transpose_round(i):
+            grouped = stage.tile([P, S_ROUND * DM], BF16, align_bytes=64, name="grouped")
+            words = grouped[:].bitcast(F32)
+            for j in range(S_ROUND):
+                s = i * S_ROUND + j
+                rows = key_rows[s // S_LOAD][:].bitcast(F32)
+                first = (s % S_LOAD) * WORDS
+                bank = transpose_rows(nc, banks, ident, rows[:, first : first + WORDS])
+                nc.scalar.copy(
+                    out=words[:, j * WORDS : (j + 1) * WORDS].rearrange(
+                        "p (g r u) -> p g r u", g=PASSES, u=HALVES
+                    ),
+                    in_=by_pass_row_half(bank),
+                )
+            grouped_of[i] = grouped
+
+        def quantise_round(i):
+            codes = stage.tile([P, S_ROUND * PASSES * P], U32, align_bytes=64, name="codes")
+            scales = stage.tile([P, S_ROUND * PASSES * P], U8, align_bytes=64, name="scales")
+            nc.vector.quantize_mx(out=codes[:].bitcast(FP8X4), scales=scales[:], in_=grouped_of[i][:])
+            codes_of[i] = (codes, scales)
+
+        def project_round(i, wk_codes, wk_scales):
+            codes, scales = codes_of[i]
+            acc_of[i] = []
+            for half in range(S_ROUND // S_BANK):
+                acc = sums.tile([P, S_BANK * DP], F32, name="acc")
+                for j in range(S_BANK):
+                    first_col = (half * S_BANK + j) * PASSES * P
+                    project(acc[:, j * DP : (j + 1) * DP], codes, scales, first_col, wk_codes, wk_scales)
+                acc_of[i].append(acc)
+
+        def score_round(i, qp):
+            prod = stage.tile([P, S_ROUND * DP], F32, name="prod")
+            for half, acc in enumerate(acc_of[i]):
+                nc.vector.tensor_tensor(
+                    out=prod[:, half * S_BANK * DP : (half + 1) * S_BANK * DP].rearrange(
+                        "p (s c) -> p s c", s=S_BANK
+                    ),
+                    in0=acc[:].rearrange("p (s c) -> p s c", s=S_BANK),
+                    in1=qp[:].unsqueeze(1).to_broadcast([P, S_BANK, DP]),
+                    op=ALU.mult,
+                )
+            nc.vector.tensor_reduce(
+                out=dot[:, :, i * S_ROUND : (i + 1) * S_ROUND],
+                in_=prod[:].rearrange("p (s h j) -> p h s j", s=S_ROUND, h=H),
+                axis=AXIS.X,
+                op=ALU.add,
+            )
+
+        transpose_round(0)
+        wk_codes, wk_scales = quantise_weight(wk_rows, "wk")
+        transpose_round(1)
+        quantise_round(0)
+        project_round(0, wk_codes, wk_scales)
+        qp = project_query()
+        for i in range(2, ROUNDS):
+            transpose_round(i)
+            quantise_round(i - 1)
+            project_round(i - 1, wk_codes, wk_scales)
+            score_round(i - 2, qp)
+        quantise_round(ROUNDS - 1)
+        project_round(ROUNDS - 1, wk_codes, wk_scales)
+        score_round(ROUNDS - 2, qp)
+        score_round(ROUNDS - 1, qp)
+
+        neg_max = const.tile([P, H], F32)
+        nc.vector.tensor_reduce(out=neg_max[:], in_=dot[:], axis=AXIS.X, op=ALU.max, negate=True)
+        expd = const.tile([P, H, SL], F32)
+        exp_sum = const.tile([P, H], F32)
+        for h in range(H):
+            nc.scalar.activation(
+                out=expd[:, h, :],
+                in_=dot[:, h, :],
+                func=ACT.Exp,
+                bias=neg_max[:, h : h + 1],
+                scale=1.0,
+                accum_out=exp_sum[:, h : h + 1],
+            )
+        log_sum = const.tile([P, H], F32)
+        nc.scalar.activation(out=log_sum[:], in_=exp_sum[:], func=ACT.Ln)
+        shift = const.tile([P, H], F32)
+        nc.vector.tensor_tensor(out=shift[:], in0=log_sum[:], in1=neg_max[:], op=ALU.subtract)
+        nc.vector.tensor_tensor(
+            out=result[:, : H * SL].rearrange("p (h s) -> p h s", h=H),
+            in0=dot[:],
+            in1=shift[:].unsqueeze(2).to_broadcast([P, H, SL]),
+            op=ALU.subtract,
+        )
+
+        flipped = banks.tile([P, H, P], F32, name="bank")
+        for h in range(H):
+            nc.tensor.transpose(flipped[:, h, :], result[:, h * SL : h * SL + P], ident[:])
+        rows_out = const.tile([P, BS, H], F32)
+        nc.vector.tensor_copy(out=rows_out[:], in_=flipped[:].rearrange("p h b -> p b h"))
+        nc.sync.dma_start(
+            out=out.rearrange("s b h -> s (b h)"),
+            in_=rows_out[:SL].rearrange("s b h -> s (b h)"),
+        )

@@ -62,22 +62,19 @@ def tile_multiheadattention_pa_t_kernel(tc, query, keys, Wq, Wk, out):
                 )
                 key_rows.append(rows)
 
-        loads_per_round = S_ROUND // S_LOAD
         wk_rows = const.tile([P, (DP // P) * DM], BF16)
         wq_rows = const.tile([P, (DP // P) * DM], BF16)
         q_rows = const.tile([P, DM], BF16)
-        load_keys(0, loads_per_round)
-        nc.sync.dma_start(
-            out=wk_rows[:].rearrange("p (r k) -> p r k", k=DM),
-            in_=Wk.rearrange("(r p) k -> p r k", p=P),
-        )
-        load_keys(loads_per_round, 2 * loads_per_round)
         nc.sync.dma_start(out=q_rows[:], in_=query)
         nc.sync.dma_start(
             out=wq_rows[:].rearrange("p (r k) -> p r k", k=DM),
             in_=Wq.rearrange("(r p) k -> p r k", p=P),
         )
-        load_keys(2 * loads_per_round, SL // S_LOAD)
+        nc.sync.dma_start(
+            out=wk_rows[:].rearrange("p (r k) -> p r k", k=DM),
+            in_=Wk.rearrange("(r p) k -> p r k", p=P),
+        )
+        load_keys(0, SL // S_LOAD)
 
         ident = const.tile([P, P], F32)
         make_identity(nc, ident[:])
@@ -96,7 +93,7 @@ def tile_multiheadattention_pa_t_kernel(tc, query, keys, Wq, Wk, out):
             )
             for r in range(DP // P):
                 bank = transpose_rows(nc, banks, ident, w_rows[:].bitcast(F32)[:, r * WORDS : (r + 1) * WORDS])
-                nc.vector.tensor_copy(out=words[:, :, r, :, :], in_=by_pass_row_half(bank))
+                nc.scalar.copy(out=words[:, :, r, :, :], in_=by_pass_row_half(bank))
             codes = const.tile([P, PASSES * DP], U32, align_bytes=64, name=name + "_codes")
             scales = const.tile([P, PASSES * DP], U8, align_bytes=64, name=name + "_scales")
             nc.vector.quantize_mx(out=codes[:].bitcast(FP8X4), scales=scales[:], in_=grouped[:])
@@ -116,19 +113,21 @@ def tile_multiheadattention_pa_t_kernel(tc, query, keys, Wq, Wk, out):
                     stop=(g == PASSES - 1),
                 )
 
-        def project_query():
-            wq_codes, wq_scales = quantise_weight(wq_rows, "wq")
+        def quantise_query():
             grouped = const.tile([P, DM], BF16, align_bytes=64, name="q_grouped")
             bank = transpose_rows(nc, banks, ident, q_rows[:].bitcast(F32))
-            nc.vector.tensor_copy(
+            nc.scalar.copy(
                 out=grouped[:].bitcast(F32).rearrange("p (g r u) -> p g r u", g=PASSES, u=HALVES),
                 in_=by_pass_row_half(bank),
             )
             codes = const.tile([P, PASSES * P], U32, align_bytes=64, name="q_codes")
             scales = const.tile([P, PASSES * P], U8, align_bytes=64, name="q_scales")
             nc.vector.quantize_mx(out=codes[:].bitcast(FP8X4), scales=scales[:], in_=grouped[:])
+            return codes, scales
+
+        def project_query(q_codes, q_scales, wq_codes, wq_scales):
             acc = sums.tile([P, S_BANK * DP], F32, name="acc")
-            project(acc[:, :DP], codes, scales, 0, wq_codes, wq_scales)
+            project(acc[:, :DP], q_codes, q_scales, 0, wq_codes, wq_scales)
             qp = const.tile([P, DP], F32)
             nc.scalar.mul(out=qp[:], in_=acc[:, :DP], mul=1.0 / math.sqrt(NH))
             return qp
@@ -136,6 +135,8 @@ def tile_multiheadattention_pa_t_kernel(tc, query, keys, Wq, Wk, out):
         grouped_of = {}
         codes_of = {}
         acc_of = {}
+        prod_of = {}
+        folded_of = {}
 
         def transpose_round(i):
             grouped = stage.tile([P, S_ROUND * DM], BF16, align_bytes=64, name="grouped")
@@ -169,7 +170,7 @@ def tile_multiheadattention_pa_t_kernel(tc, query, keys, Wq, Wk, out):
                     project(acc[:, j * DP : (j + 1) * DP], codes, scales, first_col, wk_codes, wk_scales)
                 acc_of[i].append(acc)
 
-        def score_round(i, qp):
+        def multiply_round(i, qp):
             prod = stage.tile([P, S_ROUND * DP], F32, name="prod")
             for half, acc in enumerate(acc_of[i]):
                 nc.vector.tensor_tensor(
@@ -180,28 +181,47 @@ def tile_multiheadattention_pa_t_kernel(tc, query, keys, Wq, Wk, out):
                     in1=qp[:].unsqueeze(1).to_broadcast([P, S_BANK, DP]),
                     op=ALU.mult,
                 )
+            prod_of[i] = prod
+
+        def fold_round(i):
+            folded = stage.tile([P, S_ROUND * DP // 2], F32, name="folded")
+            halves = prod_of[i][:].rearrange("p (g t j) -> p g t j", t=2, j=NH // 2)
+            nc.gpsimd.tensor_tensor(
+                out=folded[:].rearrange("p (g j) -> p g j", j=NH // 2),
+                in0=halves[:, :, 0, :],
+                in1=halves[:, :, 1, :],
+                op=ALU.add,
+            )
+            folded_of[i] = folded
+
+        def sum_round(i):
             nc.vector.tensor_reduce(
                 out=dot[:, :, i * S_ROUND : (i + 1) * S_ROUND],
-                in_=prod[:].rearrange("p (s h j) -> p h s j", s=S_ROUND, h=H),
+                in_=folded_of[i][:].rearrange("p (s h j) -> p h s j", s=S_ROUND, h=H),
                 axis=AXIS.X,
                 op=ALU.add,
             )
 
-        transpose_round(0)
+        def live(i):
+            return 0 <= i < ROUNDS
+
+        q_codes, q_scales = quantise_query()
+        wq_codes, wq_scales = quantise_weight(wq_rows, "wq")
         wk_codes, wk_scales = quantise_weight(wk_rows, "wk")
-        transpose_round(1)
-        quantise_round(0)
-        project_round(0, wk_codes, wk_scales)
-        qp = project_query()
-        for i in range(2, ROUNDS):
-            transpose_round(i)
-            quantise_round(i - 1)
-            project_round(i - 1, wk_codes, wk_scales)
-            score_round(i - 2, qp)
-        quantise_round(ROUNDS - 1)
-        project_round(ROUNDS - 1, wk_codes, wk_scales)
-        score_round(ROUNDS - 2, qp)
-        score_round(ROUNDS - 1, qp)
+        transpose_round(0)
+        qp = project_query(q_codes, q_scales, wq_codes, wq_scales)
+        for step in range(1, ROUNDS + 4):
+            if live(step):
+                transpose_round(step)
+            if live(step - 3):
+                multiply_round(step - 3, qp)
+            if live(step - 1):
+                quantise_round(step - 1)
+                project_round(step - 1, wk_codes, wk_scales)
+            if live(step - 3):
+                fold_round(step - 3)
+            if live(step - 4):
+                sum_round(step - 4)
 
         neg_max = const.tile([P, H], F32)
         nc.vector.tensor_reduce(out=neg_max[:], in_=dot[:], axis=AXIS.X, op=ALU.max, negate=True)

@@ -26,6 +26,7 @@ S_LOAD = 2
 S_ROUND = 4
 ROUNDS = SL // S_ROUND
 S_BANK = 512 // DP
+H_VECTOR = 3
 
 FLOPS = 2 * (SL + 1) * BS * DM * DP
 
@@ -78,10 +79,6 @@ def tile_multiheadattention_pa_t_kernel(tc, query, keys, Wq, Wk, out):
 
         ident = const.tile([P, P], F32)
         make_identity(nc, ident[:])
-        one = const.tile([P, 1], F32)
-        nc.vector.memset(one[:], 1.0)
-        warm = const.tile([P, 1], F32)
-        nc.scalar.activation(out=warm[:], in_=one[:], func=ACT.Ln)
         dot = const.tile([P, H, SL], F32)
         result = const.tile([P, (H + 1) * SL], F32)
         nc.gpsimd.memset(result[:, H * SL :], 0.0)
@@ -195,12 +192,23 @@ def tile_multiheadattention_pa_t_kernel(tc, query, keys, Wq, Wk, out):
             folded_of[i] = folded
 
         def sum_round(i):
+            by_head = folded_of[i][:].rearrange("p (s h j) -> p h s j", s=S_ROUND, h=H)
             nc.vector.tensor_reduce(
-                out=dot[:, :, i * S_ROUND : (i + 1) * S_ROUND],
-                in_=folded_of[i][:].rearrange("p (s h j) -> p h s j", s=S_ROUND, h=H),
+                out=dot[:, :H_VECTOR, i * S_ROUND : (i + 1) * S_ROUND],
+                in_=by_head[:, :H_VECTOR],
                 axis=AXIS.X,
                 op=ALU.add,
             )
+            unused = stage.tile([P, H - H_VECTOR, S_ROUND, NH // 2], F32, name="unused")
+            for h in range(H_VECTOR, H):
+                for j in range(S_ROUND):
+                    s = i * S_ROUND + j
+                    nc.scalar.activation(
+                        out=unused[:, h - H_VECTOR, j, :],
+                        in_=by_head[:, h, j, :],
+                        func=ACT.Copy,
+                        accum_out=dot[:, h, s : s + 1],
+                    )
 
         def live(i):
             return 0 <= i < ROUNDS

@@ -23,10 +23,13 @@ WORDS = DM // 2
 CHUNKS = WORDS // P
 HALVES = CHUNKS // PASSES
 S_LOAD = 2
-S_ROUND = 4
+S_ROUND = 2
 ROUNDS = SL // S_ROUND
 S_BANK = 512 // DP
 H_VECTOR = 3
+LAG_PROJECT = 2
+LAG_MULTIPLY = 4
+LAG_SUM = 5
 
 FLOPS = 2 * (SL + 1) * BS * DM * DP
 
@@ -47,7 +50,7 @@ def tile_multiheadattention_pa_t_kernel(tc, query, keys, Wq, Wk, out):
     with ExitStack() as ctx:
         const = ctx.enter_context(tc.tile_pool(name="const", bufs=1))
         resident = ctx.enter_context(tc.tile_pool(name="resident", bufs=SL // S_LOAD))
-        stage = ctx.enter_context(tc.tile_pool(name="stage", bufs=3))
+        stage = ctx.enter_context(tc.tile_pool(name="stage", bufs=4))
         banks = ctx.enter_context(tc.psum_pool(name="banks", bufs=4))
         sums = ctx.enter_context(tc.psum_pool(name="sums", bufs=4))
         ctx.enter_context(tc.manual_schedule())
@@ -218,18 +221,18 @@ def tile_multiheadattention_pa_t_kernel(tc, query, keys, Wq, Wk, out):
         wk_codes, wk_scales = quantise_weight(wk_rows, "wk")
         transpose_round(0)
         qp = project_query(q_codes, q_scales, wq_codes, wq_scales)
-        for step in range(1, ROUNDS + 4):
+        for step in range(1, ROUNDS + LAG_SUM):
             if live(step):
                 transpose_round(step)
-            if live(step - 3):
-                multiply_round(step - 3, qp)
-            if live(step - 1):
-                quantise_round(step - 1)
-                project_round(step - 1, wk_codes, wk_scales)
-            if live(step - 3):
-                fold_round(step - 3)
-            if live(step - 4):
-                sum_round(step - 4)
+            if live(step - LAG_MULTIPLY):
+                multiply_round(step - LAG_MULTIPLY, qp)
+            if live(step - LAG_PROJECT):
+                quantise_round(step - LAG_PROJECT)
+                project_round(step - LAG_PROJECT, wk_codes, wk_scales)
+            if live(step - LAG_MULTIPLY):
+                fold_round(step - LAG_MULTIPLY)
+            if live(step - LAG_SUM):
+                sum_round(step - LAG_SUM)
 
         neg_max = const.tile([P, H], F32)
         nc.vector.tensor_reduce(out=neg_max[:], in_=dot[:], axis=AXIS.X, op=ALU.max, negate=True)

@@ -184,34 +184,34 @@ def tile_multiheadattention_pa_t_kernel(tc, query, keys, Wq, Wk, out):
             prod_of[i] = prod
 
         def fold_round(i):
-            folded = stage.tile([P, S_ROUND * DP // 2], F32, name="folded")
-            halves = prod_of[i][:].rearrange("p (g t j) -> p g t j", t=2, j=NH // 2)
+            halves = prod_of[i][:].rearrange("p (s h t j) -> p s h t j", s=S_ROUND, h=H, t=2)
+            folded = stage.tile([P, S_ROUND, H_VECTOR, NH // 2], F32, name="folded")
             nc.gpsimd.tensor_tensor(
-                out=folded[:].rearrange("p (g j) -> p g j", j=NH // 2),
-                in0=halves[:, :, 0, :],
-                in1=halves[:, :, 1, :],
+                out=folded[:],
+                in0=halves[:, :, :H_VECTOR, 0, :],
+                in1=halves[:, :, :H_VECTOR, 1, :],
                 op=ALU.add,
             )
             folded_of[i] = folded
-
-        def sum_round(i):
-            by_head = folded_of[i][:].rearrange("p (s h j) -> p h s j", s=S_ROUND, h=H)
-            nc.vector.tensor_reduce(
-                out=dot[:, :H_VECTOR, i * S_ROUND : (i + 1) * S_ROUND],
-                in_=by_head[:, :H_VECTOR],
-                axis=AXIS.X,
-                op=ALU.add,
-            )
-            unused = stage.tile([P, H - H_VECTOR, S_ROUND, NH // 2], F32, name="unused")
-            for h in range(H_VECTOR, H):
-                for j in range(S_ROUND):
-                    s = i * S_ROUND + j
+            by_head = prod_of[i][:].rearrange("p (s h j) -> p s h j", s=S_ROUND, h=H)
+            unused = stage.tile([P, S_ROUND, H - H_VECTOR, NH], F32, name="unused")
+            for j in range(S_ROUND):
+                s = i * S_ROUND + j
+                for h in range(H_VECTOR, H):
                     nc.scalar.activation(
-                        out=unused[:, h - H_VECTOR, j, :],
-                        in_=by_head[:, h, j, :],
+                        out=unused[:, j, h - H_VECTOR, :],
+                        in_=by_head[:, j, h, :],
                         func=ACT.Copy,
                         accum_out=dot[:, h, s : s + 1],
                     )
+
+        def sum_round(i):
+            nc.vector.tensor_reduce(
+                out=dot[:, :H_VECTOR, i * S_ROUND : (i + 1) * S_ROUND],
+                in_=folded_of[i][:].rearrange("p s h j -> p h s j"),
+                axis=AXIS.X,
+                op=ALU.add,
+            )
 
         def live(i):
             return 0 <= i < ROUNDS

@@ -27,6 +27,7 @@ S_ROUND = 2
 ROUNDS = SL // S_ROUND
 S_BANK = 512 // DP
 H_VECTOR = 3
+T_RUN = 2
 LAG_PROJECT = 2
 LAG_MULTIPLY = 4
 LAG_SUM = 5
@@ -219,11 +220,11 @@ def tile_multiheadattention_pa_t_kernel(tc, query, keys, Wq, Wk, out):
         q_codes, q_scales = quantise_query()
         wq_codes, wq_scales = quantise_weight(wq_rows, "wq")
         wk_codes, wk_scales = quantise_weight(wk_rows, "wk")
-        transpose_round(0)
         qp = project_query(q_codes, q_scales, wq_codes, wq_scales)
-        for step in range(1, ROUNDS + LAG_SUM):
-            if live(step):
-                transpose_round(step)
+        for step in range(ROUNDS + LAG_SUM):
+            if live(step) and step % T_RUN == 0:
+                for i in range(step, step + T_RUN):
+                    transpose_round(i)
             if live(step - LAG_MULTIPLY):
                 multiply_round(step - LAG_MULTIPLY, qp)
             if live(step - LAG_PROJECT):

import math
from contextlib import ExitStack

import concourse.mybir as mybir
from concourse.masks import make_identity

F32 = mybir.dt.float32
BF16 = mybir.dt.bfloat16
U32 = mybir.dt.uint32
U8 = mybir.dt.uint8
FP8X4 = mybir.dt.float8_e4m3fn_x4
ALU = mybir.AluOpType
ACT = mybir.ActivationFunctionType
AXIS = mybir.AxisListType

SL, BS, DM, H, NH = 64, 128, 1024, 4, 64
DP = H * NH
P = 128
PACK = 4
K_PASS = P * PACK
PASSES = DM // K_PASS
WORDS = DM // 2
CHUNKS = WORDS // P
HALVES = CHUNKS // PASSES
S_LOAD = 2
S_ROUND = 2
ROUNDS = SL // S_ROUND
S_BANK = 512 // DP
H_VECTOR = 3
T_RUN = 2
LAG_PROJECT = 2
LAG_MULTIPLY = 4
LAG_SUM = 5

FLOPS = 2 * (SL + 1) * BS * DM * DP


def transpose_rows(nc, banks, ident, row_words):
    bank = banks.tile([P, CHUNKS, P], F32)
    for c in range(CHUNKS):
        nc.tensor.transpose(bank[:, c, :], row_words[:, c * P : (c + 1) * P], ident[:])
    return bank


def by_pass_row_half(bank):
    return bank[:].rearrange("p (g u) r -> p g r u", u=HALVES)


def tile_multiheadattention_pa_t_kernel(tc, query, keys, Wq, Wk, out):
    nc = tc.nc
    with ExitStack() as ctx:
        const = ctx.enter_context(tc.tile_pool(name="const", bufs=1))
        resident = ctx.enter_context(tc.tile_pool(name="resident", bufs=SL // S_LOAD))
        stage = ctx.enter_context(tc.tile_pool(name="stage", bufs=4))
        banks = ctx.enter_context(tc.psum_pool(name="banks", bufs=4))
        sums = ctx.enter_context(tc.psum_pool(name="sums", bufs=4))
        ctx.enter_context(tc.manual_schedule())

        key_rows = []

        def load_keys(first, last):
            for i in range(first, last):
                rows = resident.tile([P, S_LOAD * DM], BF16, name="rows")
                nc.sync.dma_start(
                    out=rows[:].rearrange("b (s k) -> b s k", s=S_LOAD),
                    in_=keys[i * S_LOAD : (i + 1) * S_LOAD].rearrange("s b k -> b s k"),
                )
                key_rows.append(rows)

        wk_rows = const.tile([P, (DP // P) * DM], BF16)
        wq_rows = const.tile([P, (DP // P) * DM], BF16)
        q_rows = const.tile([P, DM], BF16)
        nc.sync.dma_start(out=q_rows[:], in_=query)
        nc.sync.dma_start(
            out=wq_rows[:].rearrange("p (r k) -> p r k", k=DM),
            in_=Wq.rearrange("(r p) k -> p r k", p=P),
        )
        nc.sync.dma_start(
            out=wk_rows[:].rearrange("p (r k) -> p r k", k=DM),
            in_=Wk.rearrange("(r p) k -> p r k", p=P),
        )
        load_keys(0, SL // S_LOAD)

        ident = const.tile([P, P], F32)
        make_identity(nc, ident[:])
        dot = const.tile([P, H, SL], F32)
        result = const.tile([P, (H + 1) * SL], F32)
        nc.gpsimd.memset(result[:, H * SL :], 0.0)

        def quantise_weight(w_rows, name):
            grouped = const.tile([P, PASSES * DP * PACK], BF16, align_bytes=64, name=name + "_grouped")
            words = grouped[:].bitcast(F32).rearrange(
                "p (g r c u) -> p g r c u", g=PASSES, r=DP // P, u=HALVES
            )
            for r in range(DP // P):
                bank = transpose_rows(nc, banks, ident, w_rows[:].bitcast(F32)[:, r * WORDS : (r + 1) * WORDS])
                nc.scalar.copy(out=words[:, :, r, :, :], in_=by_pass_row_half(bank))
            codes = const.tile([P, PASSES * DP], U32, align_bytes=64, name=name + "_codes")
            scales = const.tile([P, PASSES * DP], U8, align_bytes=64, name=name + "_scales")
            nc.vector.quantize_mx(out=codes[:].bitcast(FP8X4), scales=scales[:], in_=grouped[:])
            return codes, scales

        def project(acc, row_codes, row_scales, first_col, w_codes, w_scales):
            for g in range(PASSES):
                rows = slice(first_col + g * P, first_col + (g + 1) * P)
                chans = slice(g * DP, (g + 1) * DP)
                nc.tensor.matmul_mx(
                    out=acc,
                    lhsT=row_codes[:, rows].bitcast(FP8X4),
                    lhsT_scale=row_scales[:, rows],
                    rhs=w_codes[:, chans].bitcast(FP8X4),
                    rhs_scale=w_scales[:, chans],
                    start=(g == 0),
                    stop=(g == PASSES - 1),
                )

        def quantise_query():
            grouped = const.tile([P, DM], BF16, align_bytes=64, name="q_grouped")
            bank = transpose_rows(nc, banks, ident, q_rows[:].bitcast(F32))
            nc.scalar.copy(
                out=grouped[:].bitcast(F32).rearrange("p (g r u) -> p g r u", g=PASSES, u=HALVES),
                in_=by_pass_row_half(bank),
            )
            codes = const.tile([P, PASSES * P], U32, align_bytes=64, name="q_codes")
            scales = const.tile([P, PASSES * P], U8, align_bytes=64, name="q_scales")
            nc.vector.quantize_mx(out=codes[:].bitcast(FP8X4), scales=scales[:], in_=grouped[:])
            return codes, scales

        def project_query(q_codes, q_scales, wq_codes, wq_scales):
            acc = sums.tile([P, S_BANK * DP], F32, name="acc")
            project(acc[:, :DP], q_codes, q_scales, 0, wq_codes, wq_scales)
            qp = const.tile([P, DP], F32)
            nc.scalar.mul(out=qp[:], in_=acc[:, :DP], mul=1.0 / math.sqrt(NH))
            return qp

        grouped_of = {}
        codes_of = {}
        acc_of = {}
        prod_of = {}
        folded_of = {}

        def transpose_round(i):
            grouped = stage.tile([P, S_ROUND * DM], BF16, align_bytes=64, name="grouped")
            words = grouped[:].bitcast(F32)
            for j in range(S_ROUND):
                s = i * S_ROUND + j
                rows = key_rows[s // S_LOAD][:].bitcast(F32)
                first = (s % S_LOAD) * WORDS
                bank = transpose_rows(nc, banks, ident, rows[:, first : first + WORDS])
                nc.scalar.copy(
                    out=words[:, j * WORDS : (j + 1) * WORDS].rearrange(
                        "p (g r u) -> p g r u", g=PASSES, u=HALVES
                    ),
                    in_=by_pass_row_half(bank),
                )
            grouped_of[i] = grouped

        def quantise_round(i):
            codes = stage.tile([P, S_ROUND * PASSES * P], U32, align_bytes=64, name="codes")
            scales = stage.tile([P, S_ROUND * PASSES * P], U8, align_bytes=64, name="scales")
            nc.vector.quantize_mx(out=codes[:].bitcast(FP8X4), scales=scales[:], in_=grouped_of[i][:])
            codes_of[i] = (codes, scales)

        def project_round(i, wk_codes, wk_scales):
            codes, scales = codes_of[i]
            acc_of[i] = []
            for half in range(S_ROUND // S_BANK):
                acc = sums.tile([P, S_BANK * DP], F32, name="acc")
                for j in range(S_BANK):
                    first_col = (half * S_BANK + j) * PASSES * P
                    project(acc[:, j * DP : (j + 1) * DP], codes, scales, first_col, wk_codes, wk_scales)
                acc_of[i].append(acc)

        def multiply_round(i, qp):
            prod = stage.tile([P, S_ROUND * DP], F32, name="prod")
            for half, acc in enumerate(acc_of[i]):
                nc.vector.tensor_tensor(
                    out=prod[:, half * S_BANK * DP : (half + 1) * S_BANK * DP].rearrange(
                        "p (s c) -> p s c", s=S_BANK
                    ),
                    in0=acc[:].rearrange("p (s c) -> p s c", s=S_BANK),
                    in1=qp[:].unsqueeze(1).to_broadcast([P, S_BANK, DP]),
                    op=ALU.mult,
                )
            prod_of[i] = prod

        def fold_round(i):
            halves = prod_of[i][:].rearrange("p (s h t j) -> p s h t j", s=S_ROUND, h=H, t=2)
            folded = stage.tile([P, S_ROUND, H_VECTOR, NH // 2], F32, name="folded")
            nc.gpsimd.tensor_tensor(
                out=folded[:],
                in0=halves[:, :, :H_VECTOR, 0, :],
                in1=halves[:, :, :H_VECTOR, 1, :],
                op=ALU.add,
            )
            folded_of[i] = folded
            by_head = prod_of[i][:].rearrange("p (s h j) -> p s h j", s=S_ROUND, h=H)
            unused = stage.tile([P, S_ROUND, H - H_VECTOR, NH], F32, name="unused")
            for j in range(S_ROUND):
                s = i * S_ROUND + j
                for h in range(H_VECTOR, H):
                    nc.scalar.activation(
                        out=unused[:, j, h - H_VECTOR, :],
                        in_=by_head[:, j, h, :],
                        func=ACT.Copy,
                        accum_out=dot[:, h, s : s + 1],
                    )

        def sum_round(i):
            nc.vector.tensor_reduce(
                out=dot[:, :H_VECTOR, i * S_ROUND : (i + 1) * S_ROUND],
                in_=folded_of[i][:].rearrange("p s h j -> p h s j"),
                axis=AXIS.X,
                op=ALU.add,
            )

        def live(i):
            return 0 <= i < ROUNDS

        q_codes, q_scales = quantise_query()
        wq_codes, wq_scales = quantise_weight(wq_rows, "wq")
        wk_codes, wk_scales = quantise_weight(wk_rows, "wk")
        qp = project_query(q_codes, q_scales, wq_codes, wq_scales)
        for step in range(ROUNDS + LAG_SUM):
            if live(step) and step % T_RUN == 0:
                for i in range(step, step + T_RUN):
                    transpose_round(i)
            if live(step - LAG_MULTIPLY):
                multiply_round(step - LAG_MULTIPLY, qp)
            if live(step - LAG_PROJECT):
                quantise_round(step - LAG_PROJECT)
                project_round(step - LAG_PROJECT, wk_codes, wk_scales)
            if live(step - LAG_MULTIPLY):
                fold_round(step - LAG_MULTIPLY)
            if live(step - LAG_SUM):
                sum_round(step - LAG_SUM)

        neg_max = const.tile([P, H], F32)
        nc.vector.tensor_reduce(out=neg_max[:], in_=dot[:], axis=AXIS.X, op=ALU.max, negate=True)
        expd = const.tile([P, H, SL], F32)
        exp_sum = const.tile([P, H], F32)
        for h in range(H):
            nc.scalar.activation(
                out=expd[:, h, :],
                in_=dot[:, h, :],
                func=ACT.Exp,
                bias=neg_max[:, h : h + 1],
                scale=1.0,
                accum_out=exp_sum[:, h : h + 1],
            )
        log_sum = const.tile([P, H], F32)
        nc.scalar.activation(out=log_sum[:], in_=exp_sum[:], func=ACT.Ln)
        shift = const.tile([P, H], F32)
        nc.vector.tensor_tensor(out=shift[:], in0=log_sum[:], in1=neg_max[:], op=ALU.subtract)
        nc.vector.tensor_tensor(
            out=result[:, : H * SL].rearrange("p (h s) -> p h s", h=H),
            in0=dot[:],
            in1=shift[:].unsqueeze(2).to_broadcast([P, H, SL]),
            op=ALU.subtract,
        )

        flipped = banks.tile([P, H, P], F32, name="bank")
        for h in range(H):
            nc.tensor.transpose(flipped[:, h, :], result[:, h * SL : h * SL + P], ident[:])
        rows_out = const.tile([P, BS, H], F32)
        nc.vector.tensor_copy(out=rows_out[:], in_=flipped[:].rearrange("p h b -> p b h"))
        nc.sync.dma_start(
            out=out.rearrange("s b h -> s (b h)"),
            in_=rows_out[:SL].rearrange("s b h -> s (b h)"),
        )
